import numpy as np
import ml_dtypes


def mxq(x, axis, fmt="e4m3"):
    dtype, down = {"e4m3": (ml_dtypes.float8_e4m3fn, 7), "e5m2": (ml_dtypes.float8_e5m2, 14)}[fmt]
    v = np.moveaxis(np.asarray(x, np.float32).astype(ml_dtypes.bfloat16).astype(np.float64), axis, -1)
    blocks = v.reshape(v.shape[:-1] + (-1, 32))
    amax = np.abs(blocks).max(-1, keepdims=True)
    byte = np.maximum(np.where(amax > 0, np.frexp(amax)[1] - 1 + 127, 0) - down, 1)
    scale = np.exp2(byte - 127.0)
    codes = (blocks / scale).astype(np.float32).astype(dtype).astype(np.float64)
    return np.moveaxis((codes * scale).reshape(v.shape), -1, axis)


WIDE = False


def mx_kscale(k):
    if not WIDE:
        return np.ones(k)
    levels = np.array([10, -10, 5, -5, 0])
    a = np.random.permutation(np.resize(levels, k // 512 * 4)).reshape(k // 512, 4)
    idx = np.arange(k)
    return np.exp2(a[idx // 512, idx % 128 // 32])


BF16 = ml_dtypes.bfloat16


def bf(x):
    return np.asarray(x, np.float32).astype(BF16)


def f64(x):
    return np.asarray(x).astype(np.float64)


E2M1 = np.array([0.0, 0.5, 1.0, 1.5, 2.0, 3.0, 4.0, 6.0, -0.0, -0.5, -1.0, -1.5, -2.0, -3.0, -4.0, -6.0])


def pack_weight(w, fmt):
    k, n = w.shape
    w = f64(bf(w)).reshape(k // 32, 32, n)
    amax = np.abs(w).max(1)
    if fmt == "e4m3":
        byte = np.frexp(amax)[1] - 1 + 127 - 7
    else:
        mant, ex = np.frexp(amax / 6.0)
        byte = np.where(mant > 0.5, ex, ex - 1) + 127
    byte = np.clip(np.where(amax > 0, byte, 1), 1, 254)
    scaled = (w * np.exp2(127.0 - byte)[:, None, :]).reshape(k, n).astype(np.float32)
    by_word = np.ascontiguousarray(scaled.reshape(k // 512, 128, 4, n).transpose(0, 1, 3, 2))
    if fmt == "e4m3":
        words = by_word.astype(ml_dtypes.float8_e4m3fn).view(np.uint8)
    else:
        c = by_word.astype(ml_dtypes.float4_e2m1fn).view(np.uint8) & 0xF
        words = c[..., 0::2] | (c[..., 1::2] << 4)
    return np.ascontiguousarray(words), np.ascontiguousarray(byte.astype(np.uint8).reshape(k // 512, 16, n))


def unpack_weight(words, scales, fmt):
    g, p, n, _ = words.shape
    if fmt == "e4m3":
        vals = np.ascontiguousarray(words).view(ml_dtypes.float8_e4m3fn).astype(np.float64)
    else:
        nib = np.empty((g, p, n, 4), np.uint8)
        nib[..., 0::2] = words & 0xF
        nib[..., 1::2] = words >> 4
        vals = E2M1[nib]
    vals = vals * np.repeat(np.exp2(scales.astype(np.float64) - 127.0), 8, axis=1)[..., None]
    return vals.transpose(0, 1, 3, 2).reshape(g * 512, n)


B, L0, W0, R, DIM, OUT = 4096, 16, 8, 32, 512, 128
K1 = L0 * W0
KR = R * R
EPS = 1e-5
FMT = "e4m3"


def setup_inputs():
    s2, s3 = mx_kscale(KR), mx_kscale(KR)
    rn = np.random.standard_normal
    d = {
        "x": bf(rn((B, L0, W0))),
        "km1": bf(rn((L0, W0, DIM)) / np.sqrt(K1)),
        "b1": bf(0.5 + 0.3 * rn(DIM)),
        "t2": bf(rn((B, R, R)) * s2.reshape(R, R)),
        "core2": bf(rn((R, R, DIM)) / np.sqrt(KR) / s2.reshape(R, R, 1)),
        "t3": bf(rn((B, R, R)) * s3.reshape(R, R)),
        "core3": bf(rn((R, R, DIM)) / np.sqrt(KR) / s3.reshape(R, R, 1)),
        "ln_g": bf(1.0 + 0.1 * rn(DIM)),
        "ln_b": bf(0.1 * rn(DIM)),
    }
    fc_w = rn((OUT, DIM)) / np.sqrt(DIM)
    words, scales = pack_weight(np.ascontiguousarray(fc_w.T), FMT)
    d["fc_w_words"] = words
    d["fc_w_scales"] = scales
    d["fc_b"] = bf(0.3 * rn(OUT))
    return d


def reference(x, km1, b1, t2, core2, t3, core3, ln_g, ln_b, fc_w_words, fc_w_scales, fc_b):
    o = f64(x).reshape(B, K1) @ f64(km1).reshape(K1, DIM) + f64(b1)
    o = o + (mxq(f64(t2).reshape(B, KR), 1, "e4m3") @ mxq(f64(core2).reshape(KR, DIM), 0, "e4m3"))
    o = o + (mxq(f64(t3).reshape(B, KR), 1, "e4m3") @ mxq(f64(core3).reshape(KR, DIM), 0, "e4m3"))
    mu = o.mean(-1, keepdims=True)
    var = ((o - mu) ** 2).mean(-1, keepdims=True)
    y = (o - mu) / np.sqrt(var + EPS) * f64(ln_g) + f64(ln_b)
    out = (mxq(y, 1, "e4m3") @ unpack_weight(fc_w_words, fc_w_scales, FMT)) + f64(fc_b)
    return out[:, None, :]

@@ -1,0 +1,342 @@
+from contextlib import ExitStack
+
+import concourse.mybir as mybir
+from concourse.masks import make_identity
+
+F32 = mybir.dt.float32
+BF16 = mybir.dt.bfloat16
+U32 = mybir.dt.uint32
+U8 = mybir.dt.uint8
+I32 = mybir.dt.int32
+FP8X4 = mybir.dt.float8_e4m3fn_x4
+ACT = mybir.ActivationFunctionType
+ALU = mybir.AluOpType
+
+P = 128
+PACK = 4
+ROWS, K1, KR, DIM, OUT = 4096, 128, 1024, 512, 128
+EPS = 1e-5
+TILES = ROWS // P
+CORE_PASSES = KR // (P * PACK)
+PASSES = 2 * CORE_PASSES
+LOAD_AHEAD = 4
+STORE_TILES = 4
+SCALAR_PASS = 1
+
+FLOPS = 2 * ROWS * (K1 * DIM + 2 * KR * DIM + DIM * OUT)
+
+
+def tile_pinmodel_pa_t_kernel(
+    tc, x, km1, b1, t2, core2, t3, core3, ln_g, ln_b, fc_w_words, fc_w_scales, fc_b, out
+):
+    nc = tc.nc
+    with ExitStack() as ctx:
+        ctx.enter_context(tc.manual_schedule())
+        const = ctx.enter_context(tc.tile_pool(name="const", bufs=1))
+        ring = ctx.enter_context(tc.tile_pool(name="ring", bufs=LOAD_AHEAD + 1))
+        work = ctx.enter_context(tc.tile_pool(name="work", bufs=2))
+        stats = ctx.enter_context(tc.tile_pool(name="stats", bufs=3))
+        psum = ctx.enter_context(tc.psum_pool(name="psum", bufs=1))
+
+        x_rows = x.rearrange("(p i) a b -> p i (a b)", i=TILES)
+        t_rows = {
+            "t2": t2.rearrange("(p i) a b -> p i (a b)", i=TILES),
+            "t3": t3.rearrange("(p i) a b -> p i (a b)", i=TILES),
+        }
+        out_rows = out.rearrange("(p i) o c -> p i (o c)", i=TILES)
+
+        ident_f32 = const.tile([P, P], F32, name="ident_f32")
+        make_identity(nc, ident_f32[:])
+        ident_bf16 = const.tile([P, P], BF16, name="ident_bf16")
+        make_identity(nc, ident_bf16[:])
+        eps = const.tile([P, 1], F32, name="eps")
+        nc.vector.memset(eps[:], EPS)
+        w_scales = const.tile([P, OUT], U8, name="w_scales", align_bytes=64)
+        nc.vector.memset(w_scales[:].bitcast(I32), 0)
+
+        k1_in = const.tile([P, DIM], BF16, name="k1_in")
+        nc.scalar.dma_start(out=k1_in[:], in_=km1.rearrange("a b d -> (a b) d"))
+        b1_col = const.tile([P, PACK], BF16, name="b1_col")
+        nc.scalar.dma_start(out=b1_col[:], in_=b1.rearrange("(j t) -> j t", t=PACK))
+        fcb_col = const.tile([P, 1], BF16, name="fcb_col")
+        nc.scalar.dma_start(out=fcb_col[:], in_=fc_b.rearrange("(n o) -> n o", o=1))
+        gain_col = const.tile([P, PACK], BF16, name="gain_col")
+        nc.scalar.dma_start(out=gain_col[:], in_=ln_g.rearrange("(j t) -> j t", t=PACK))
+        shift_col = const.tile([P, PACK], BF16, name="shift_col")
+        nc.scalar.dma_start(out=shift_col[:], in_=ln_b.rearrange("(j t) -> j t", t=PACK))
+        warm = const.tile([P, 1], F32, name="warm")
+        nc.scalar.activation(out=warm[:], in_=eps[:], func=ACT.Sqrt)
+
+        core_in = const.tile([P, PASSES * PACK, DIM], BF16, name="core_in")
+        for c in range(PASSES):
+            core = (core2, core3)[c // CORE_PASSES]
+            g = c % CORE_PASSES
+            halves = core.rearrange("a b d -> (a b) d").rearrange(
+                "(h q e) d -> q h (e d)", q=P, e=2
+            )
+            nc.sync.dma_start(
+                out=core_in[:, PACK * c : PACK * (c + 1), :].rearrange("q (u e) d -> q u (e d)", e=2),
+                in_=halves[:, 2 * g : 2 * g + 2, :],
+            )
+
+        handed = {}
+
+        def load_inputs(i):
+            for name in ("t2", "t3"):
+                t_in = ring.tile([P, KR], BF16, name=name + "_in")
+                nc.sync.dma_start(out=t_in[:], in_=t_rows[name][:, i, :])
+                handed[name + "_in", i] = t_in
+            x_in = ring.tile([P, K1], BF16, name="x_in")
+            nc.sync.dma_start(out=x_in[:], in_=x_rows[:, i, :])
+            handed["x_in", i] = x_in
+
+        for i in range(LOAD_AHEAD):
+            load_inputs(i)
+
+        w_words = const.tile([P, OUT], U32, name="w_words", align_bytes=64)
+        nc.sync.dma_start(
+            out=w_words[:].bitcast(I32),
+            in_=fc_w_words[0].rearrange("p n t -> p (n t)").bitcast(I32),
+        )
+        for quadrant in range(4):
+            nc.sync.dma_start(
+                out=w_scales[32 * quadrant : 32 * quadrant + 4, :].bitcast(I32),
+                in_=fc_w_scales[0, 4 * quadrant : 4 * quadrant + 4, :].bitcast(I32),
+            )
+
+        k1_cols = const.tile([P, DIM], BF16, name="k1_cols")
+        nc.gpsimd.tensor_copy(
+            out=k1_cols[:].rearrange("k (t j) -> k t j", t=PACK),
+            in_=k1_in[:].rearrange("k (j t) -> k t j", t=PACK),
+        )
+        gain = const.tile([P, PACK], F32, name="gain")
+        nc.gpsimd.tensor_copy(out=gain[:], in_=gain_col[:])
+        shift = const.tile([P, PACK], F32, name="shift")
+        nc.gpsimd.tensor_copy(out=shift[:], in_=shift_col[:])
+
+        b1_ps = psum.tile([P, DIM], F32, name="acc", bufs=2)
+        for t in range(PACK):
+            nc.tensor.matmul(
+                out=b1_ps[:, P * t : P * (t + 1)],
+                lhsT=b1_col[:, t : t + 1].to_broadcast([P, P]),
+                rhs=ident_bf16[:],
+                start=True,
+                stop=True,
+            )
+        fcb_ps = psum.tile([P, DIM], F32, name="acc", bufs=2)
+        nc.tensor.matmul(
+            out=fcb_ps[:, 0:OUT],
+            lhsT=fcb_col[:, 0:1].to_broadcast([P, P]),
+            rhs=ident_bf16[:],
+            start=True,
+            stop=True,
+        )
+
+        core_grouped = const.tile([P, PASSES, DIM, PACK], BF16, name="core_grouped", align_bytes=64)
+        core_codes = const.tile([P, PASSES, DIM], U32, name="core_codes", align_bytes=64)
+        core_scales = const.tile([P, PASSES, DIM], U8, name="core_scales", align_bytes=64)
+
+        def regroup_core(c):
+            copy = nc.scalar.copy if c == SCALAR_PASS else nc.vector.tensor_copy
+            copy(
+                out=core_grouped[:, c, :, :].rearrange("q (t j) v -> q j v t", t=PACK),
+                in_=core_in[:, PACK * c : PACK * (c + 1), :].rearrange("q v (j t) -> q j v t", t=PACK),
+            )
+
+        def quantise_core(c):
+            nc.vector.quantize_mx(
+                out=core_codes[:, c, :].bitcast(FP8X4),
+                scales=core_scales[:, c, :],
+                in_=core_grouped[:, c, :, :].rearrange("q d v -> q (d v)"),
+            )
+
+        for c in range(PASSES + 1):
+            if c < PASSES:
+                regroup_core(c)
+            if c >= 1:
+                quantise_core(c - 1)
+
+        b1_cols = const.tile([P, DIM], F32, name="b1_cols")
+        nc.scalar.copy(out=b1_cols[:], in_=b1_ps[:])
+        fc_bias = const.tile([P, OUT], F32, name="fc_bias")
+        nc.scalar.copy(out=fc_bias[:], in_=fcb_ps[:, 0:OUT])
+
+        def transpose_inputs(i):
+            for name in ("t2", "t3"):
+                pairs = handed[name + "_in", i][:].bitcast(F32)
+                flipped = psum.tile([P, CORE_PASSES, 2, P], F32, name=name + "_flipped")
+                for g in range(CORE_PASSES):
+                    for u in range(2):
+                        first = P * (2 * g + u)
+                        nc.tensor.transpose(flipped[:, g, u, :], pairs[:, first : first + P], ident_f32[:])
+                handed[name + "_flipped", i] = flipped
+            x_flipped = psum.tile([P, P], BF16, name="x_flipped")
+            nc.tensor.transpose(x_flipped[:], handed["x_in", i][:], ident_bf16[:])
+            handed["x_flipped", i] = x_flipped
+
+        def evacuate_inputs(i):
+            t_grouped = work.tile([P, PASSES, P, PACK], BF16, name="t_grouped", align_bytes=64)
+            pairs = t_grouped[:].bitcast(F32)
+            for first, name in ((0, "t2"), (CORE_PASSES, "t3")):
+                nc.scalar.copy(
+                    out=pairs[:, first : first + CORE_PASSES],
+                    in_=handed[name + "_flipped", i][:].rearrange("q g u r -> q g r u"),
+                )
+            handed["t_grouped", i] = t_grouped
+            x_cols = work.tile([P, P], BF16, name="x_cols")
+            nc.scalar.copy(out=x_cols[:], in_=handed["x_flipped", i][:])
+            handed["x_cols", i] = x_cols
+
+        def quantise_t(i):
+            t_codes = work.tile([P, PASSES * P], U32, name="t_codes", align_bytes=64)
+            t_scales = work.tile([P, PASSES * P], U8, name="t_scales", align_bytes=64)
+            nc.vector.quantize_mx(
+                out=t_codes[:].bitcast(FP8X4),
+                scales=t_scales[:],
+                in_=handed["t_grouped", i][:].rearrange("q c r v -> q (c r v)"),
+            )
+            handed["t_codes", i] = t_codes
+            handed["t_scales", i] = t_scales
+
+        def tucker_matmuls(i):
+            acc = psum.tile([P, DIM], F32, name="acc", bufs=2)
+            for c in range(PASSES):
+                samples = slice(P * c, P * (c + 1))
+                nc.tensor.matmul_mx(
+                    out=acc[:],
+                    lhsT=handed["t_codes", i][:, samples].bitcast(FP8X4),
+                    lhsT_scale=handed["t_scales", i][:, samples],
+                    rhs=core_codes[:, c, :].bitcast(FP8X4),
+                    rhs_scale=core_scales[:, c, :],
+                    start=(c == 0),
+                    stop=(c == PASSES - 1),
+                )
+            handed["acc", i] = acc
+
+        def order1_matmul(i):
+            order1 = psum.tile([P, DIM], F32, name="order1")
+            nc.tensor.matmul(out=order1[:], lhsT=handed["x_cols", i][:], rhs=k1_cols[:], start=True, stop=True)
+            handed["order1", i] = order1
+
+        def join(i):
+            partial = work.tile([P, DIM], F32, name="partial")
+            nc.vector.tensor_tensor(out=partial[:], in0=handed["order1", i][:], in1=b1_cols[:], op=ALU.add)
+            o = work.tile([P, DIM], F32, name="o")
+            row_sum = stats.tile([P, 1], F32, name="row_sum")
+            nc.vector.scalar_tensor_tensor(
+                out=o[:],
+                in0=handed["acc", i][:],
+                scalar=1.0,
+                in1=partial[:],
+                op0=ALU.mult,
+                op1=ALU.add,
+                accum_out=row_sum[:],
+            )
+            neg_mean = stats.tile([P, 1], F32, name="neg_mean")
+            nc.vector.tensor_scalar_mul(out=neg_mean[:], in0=row_sum[:], scalar1=-1.0 / DIM)
+            handed["o", i] = o
+            handed["neg_mean", i] = neg_mean
+
+        def variance(i):
+            squares = work.tile([P, DIM], BF16, name="squares")
+            sum_sq = stats.tile([P, 1], F32, name="sum_sq")
+            nc.scalar.activation(
+                out=squares[:],
+                in_=handed["o", i][:],
+                func=ACT.Square,
+                bias=handed["neg_mean", i][:],
+                scale=1.0,
+                accum_out=sum_sq[:],
+            )
+            std = stats.tile([P, 1], F32, name="std")
+            nc.scalar.activation(out=std[:], in_=sum_sq[:], func=ACT.Sqrt, bias=eps[:], scale=1.0 / DIM)
+            handed["std", i] = std
+
+        def normalise(i):
+            rstd = stats.tile([P, 1], F32, name="rstd")
+            nc.vector.reciprocal(out=rstd[:], in_=handed["std", i][:])
+            z = work.tile([P, DIM], F32, name="z")
+            nc.vector.tensor_scalar(
+                out=z[:],
+                in0=handed["o", i][:],
+                scalar1=handed["neg_mean", i][:],
+                scalar2=rstd[:],
+                op0=ALU.add,
+                op1=ALU.mult,
+            )
+            handed["z", i] = z
+
+        def transpose_z(i):
+            z_flipped = psum.tile([P, PACK, P], F32, name="z_flipped")
+            for t in range(PACK):
+                nc.tensor.transpose(z_flipped[:, t, :], handed["z", i][:, P * t : P * (t + 1)], ident_f32[:])
+            handed["z_flipped", i] = z_flipped
+
+        def affine(i):
+            y_planes = work.tile([P, PACK, P], BF16, name="y_planes")
+            for t in range(PACK):
+                nc.scalar.activation(
+                    out=y_planes[:, t, :],
+                    in_=handed["z_flipped", i][:, t, :],
+                    func=ACT.Identity,
+                    bias=shift[:, t : t + 1],
+                    scale=gain[:, t : t + 1],
+                )
+            handed["y_planes", i] = y_planes
+
+        def quantise_y(i):
+            y_grouped = work.tile([P, P, PACK], BF16, name="y_grouped", align_bytes=64)
+            nc.vector.tensor_copy(out=y_grouped[:], in_=handed["y_planes", i][:].rearrange("j t r -> j r t"))
+            y_codes = work.tile([P, P], U32, name="y_codes", align_bytes=64)
+            y_scales = work.tile([P, P], U8, name="y_scales", align_bytes=64)
+            nc.vector.quantize_mx(
+                out=y_codes[:].bitcast(FP8X4),
+                scales=y_scales[:],
+                in_=y_grouped[:].rearrange("j r t -> j (r t)"),
+            )
+            handed["y_codes", i] = y_codes
+            handed["y_scales", i] = y_scales
+
+        def head_matmul(i):
+            head = psum.tile([P, OUT], F32, name="head")
+            nc.tensor.matmul_mx(
+                out=head[:],
+                lhsT=handed["y_codes", i][:].bitcast(FP8X4),
+                lhsT_scale=handed["y_scales", i][:],
+                rhs=w_words[:].bitcast(FP8X4),
+                rhs_scale=w_scales[:],
+                start=True,
+                stop=True,
+            )
+            handed["head", i] = head
+
+        def finish(i):
+            group, place = divmod(i, STORE_TILES)
+            if place == 0:
+                handed["result", group] = work.tile([P, STORE_TILES, OUT], F32, name="result")
+            result = handed["result", group]
+            nc.vector.tensor_tensor(out=result[:, place, :], in0=handed["head", i][:], in1=fc_bias[:], op=ALU.add)
+            if place == STORE_TILES - 1:
+                nc.sync.dma_start(
+                    out=out_rows[:, STORE_TILES * group : STORE_TILES * (group + 1), :], in_=result[:]
+                )
+
+        def at(stage, i):
+            if 0 <= i < TILES:
+                stage(i)
+
+        for step in range(-1, TILES + 4):
+            at(load_inputs, step + 1 + LOAD_AHEAD)
+            at(transpose_inputs, step + 1)
+            at(transpose_z, step - 2)
+            at(join, step - 1)
+            at(evacuate_inputs, step + 1)
+            at(quantise_y, step - 3)
+            at(finish, step - 4)
+            at(tucker_matmuls, step)
+            at(head_matmul, step - 3)
+            at(order1_matmul, step)
+            at(quantise_t, step + 1)
+            at(variance, step - 1)
+            at(normalise, step - 1)
+            at(affine, step - 2)

@@ -35,7 +35,7 @@ def tile_pinmodel_pa_t_kernel(
         const = ctx.enter_context(tc.tile_pool(name="const", bufs=1))
         ring = ctx.enter_context(tc.tile_pool(name="ring", bufs=LOAD_AHEAD + 1))
         work = ctx.enter_context(tc.tile_pool(name="work", bufs=2))
-        stats = ctx.enter_context(tc.tile_pool(name="stats", bufs=3))
+        stats = ctx.enter_context(tc.tile_pool(name="stats", bufs=4))
         psum = ctx.enter_context(tc.psum_pool(name="psum", bufs=1))
 
         x_rows = x.rearrange("(p i) a b -> p i (a b)", i=TILES)
@@ -175,7 +175,7 @@ def tile_pinmodel_pa_t_kernel(
             handed["x_flipped", i] = x_flipped
 
         def evacuate_inputs(i):
-            t_grouped = work.tile([P, PASSES, P, PACK], BF16, name="t_grouped", align_bytes=64)
+            t_grouped = work.tile([P, PASSES, P, PACK], BF16, name="t_grouped", bufs=3, align_bytes=64)
             pairs = t_grouped[:].bitcast(F32)
             for first, name in ((0, "t2"), (CORE_PASSES, "t3")):
                 nc.scalar.copy(
@@ -183,7 +183,7 @@ def tile_pinmodel_pa_t_kernel(
                     in_=handed[name + "_flipped", i][:].rearrange("q g u r -> q g r u"),
                 )
             handed["t_grouped", i] = t_grouped
-            x_cols = work.tile([P, P], BF16, name="x_cols")
+            x_cols = work.tile([P, P], BF16, name="x_cols", bufs=3)
             nc.scalar.copy(out=x_cols[:], in_=handed["x_flipped", i][:])
             handed["x_cols", i] = x_cols
 
@@ -218,26 +218,32 @@ def tile_pinmodel_pa_t_kernel(
             nc.tensor.matmul(out=order1[:], lhsT=handed["x_cols", i][:], rhs=k1_cols[:], start=True, stop=True)
             handed["order1", i] = order1
 
-        def join(i):
+        def add_order1(i):
             partial = work.tile([P, DIM], F32, name="partial")
             nc.vector.tensor_tensor(out=partial[:], in0=handed["order1", i][:], in1=b1_cols[:], op=ALU.add)
-            o = work.tile([P, DIM], F32, name="o")
+            handed["partial", i] = partial
+
+        def add_tucker(i):
+            o = work.tile([P, DIM], F32, name="o", bufs=3)
             row_sum = stats.tile([P, 1], F32, name="row_sum")
             nc.vector.scalar_tensor_tensor(
                 out=o[:],
                 in0=handed["acc", i][:],
                 scalar=1.0,
-                in1=partial[:],
+                in1=handed["partial", i][:],
                 op0=ALU.mult,
                 op1=ALU.add,
                 accum_out=row_sum[:],
             )
-            neg_mean = stats.tile([P, 1], F32, name="neg_mean")
-            nc.vector.tensor_scalar_mul(out=neg_mean[:], in0=row_sum[:], scalar1=-1.0 / DIM)
             handed["o", i] = o
+            handed["row_sum", i] = row_sum
+
+        def mean(i):
+            neg_mean = stats.tile([P, 1], F32, name="neg_mean")
+            nc.vector.tensor_scalar_mul(out=neg_mean[:], in0=handed["row_sum", i][:], scalar1=-1.0 / DIM)
             handed["neg_mean", i] = neg_mean
 
-        def variance(i):
+        def sum_squares(i):
             squares = work.tile([P, DIM], BF16, name="squares")
             sum_sq = stats.tile([P, 1], F32, name="sum_sq")
             nc.scalar.activation(
@@ -248,19 +254,25 @@ def tile_pinmodel_pa_t_kernel(
                 scale=1.0,
                 accum_out=sum_sq[:],
             )
+            handed["sum_sq", i] = sum_sq
+
+        def root(i):
             std = stats.tile([P, 1], F32, name="std")
-            nc.scalar.activation(out=std[:], in_=sum_sq[:], func=ACT.Sqrt, bias=eps[:], scale=1.0 / DIM)
+            nc.scalar.activation(out=std[:], in_=handed["sum_sq", i][:], func=ACT.Sqrt, bias=eps[:], scale=1.0 / DIM)
             handed["std", i] = std
 
-        def normalise(i):
+        def inverse(i):
             rstd = stats.tile([P, 1], F32, name="rstd")
             nc.vector.reciprocal(out=rstd[:], in_=handed["std", i][:])
+            handed["rstd", i] = rstd
+
+        def normalise(i):
             z = work.tile([P, DIM], F32, name="z")
-            nc.vector.tensor_scalar(
+            nc.gpsimd.tensor_scalar(
                 out=z[:],
                 in0=handed["o", i][:],
                 scalar1=handed["neg_mean", i][:],
-                scalar2=rstd[:],
+                scalar2=handed["rstd", i][:],
                 op0=ALU.add,
                 op1=ALU.mult,
             )
@@ -284,15 +296,18 @@ def tile_pinmodel_pa_t_kernel(
                 )
             handed["y_planes", i] = y_planes
 
-        def quantise_y(i):
+        def regroup_y(i):
             y_grouped = work.tile([P, P, PACK], BF16, name="y_grouped", align_bytes=64)
             nc.vector.tensor_copy(out=y_grouped[:], in_=handed["y_planes", i][:].rearrange("j t r -> j r t"))
-            y_codes = work.tile([P, P], U32, name="y_codes", align_bytes=64)
-            y_scales = work.tile([P, P], U8, name="y_scales", align_bytes=64)
+            handed["y_grouped", i] = y_grouped
+
+        def quantise_y(i):
+            y_codes = work.tile([P, P], U32, name="y_codes", bufs=3, align_bytes=64)
+            y_scales = work.tile([P, P], U8, name="y_scales", bufs=3, align_bytes=64)
             nc.vector.quantize_mx(
                 out=y_codes[:].bitcast(FP8X4),
                 scales=y_scales[:],
-                in_=y_grouped[:].rearrange("j r t -> j (r t)"),
+                in_=handed["y_grouped", i][:].rearrange("j r t -> j (r t)"),
             )
             handed["y_codes", i] = y_codes
             handed["y_scales", i] = y_scales
@@ -325,18 +340,23 @@ def tile_pinmodel_pa_t_kernel(
             if 0 <= i < TILES:
                 stage(i)
 
-        for step in range(-1, TILES + 4):
-            at(load_inputs, step + 1 + LOAD_AHEAD)
-            at(transpose_inputs, step + 1)
-            at(transpose_z, step - 2)
-            at(join, step - 1)
-            at(evacuate_inputs, step + 1)
-            at(quantise_y, step - 3)
-            at(finish, step - 4)
-            at(tucker_matmuls, step)
-            at(head_matmul, step - 3)
-            at(order1_matmul, step)
+        for step in range(-2, TILES + 9):
+            at(load_inputs, step + 2 + LOAD_AHEAD)
+            at(transpose_inputs, step + 2)
+            at(transpose_z, step - 5)
+            at(inverse, step - 4)
+            at(normalise, step - 4)
+            at(add_order1, step - 1)
+            at(add_tucker, step - 2)
+            at(finish, step - 8)
+            at(regroup_y, step - 6)
+            at(mean, step - 2)
             at(quantise_t, step + 1)
-            at(variance, step - 1)
-            at(normalise, step - 1)
-            at(affine, step - 2)
+            at(quantise_y, step - 6)
+            at(order1_matmul, step)
+            at(tucker_matmuls, step)
+            at(head_matmul, step - 7)
+            at(evacuate_inputs, step + 2)
+            at(root, step - 3)
+            at(affine, step - 5)
+            at(sum_squares, step - 2)

@@ -54,8 +54,6 @@ def tile_pinmodel_pa_t_kernel(
         w_scales = const.tile([P, OUT], U8, name="w_scales", align_bytes=64)
         nc.vector.memset(w_scales[:].bitcast(I32), 0)
 
-        k1_in = const.tile([P, DIM], BF16, name="k1_in")
-        nc.scalar.dma_start(out=k1_in[:], in_=km1.rearrange("a b d -> (a b) d"))
         b1_col = const.tile([P, PACK], BF16, name="b1_col")
         nc.scalar.dma_start(out=b1_col[:], in_=b1.rearrange("(j t) -> j t", t=PACK))
         fcb_col = const.tile([P, 1], BF16, name="fcb_col")
@@ -78,6 +76,9 @@ def tile_pinmodel_pa_t_kernel(
                 out=core_in[:, PACK * c : PACK * (c + 1), :].rearrange("q (u e) d -> q u (e d)", e=2),
                 in_=halves[:, 2 * g : 2 * g + 2, :],
             )
+
+        k1_in = const.tile([P, DIM], BF16, name="k1_in")
+        nc.sync.dma_start(out=k1_in[:], in_=km1.rearrange("a b d -> (a b) d"))
 
         handed = {}
 
@@ -104,11 +105,6 @@ def tile_pinmodel_pa_t_kernel(
                 in_=fc_w_scales[0, 4 * quadrant : 4 * quadrant + 4, :].bitcast(I32),
             )
 
-        k1_cols = const.tile([P, DIM], BF16, name="k1_cols")
-        nc.gpsimd.tensor_copy(
-            out=k1_cols[:].rearrange("k (t j) -> k t j", t=PACK),
-            in_=k1_in[:].rearrange("k (j t) -> k t j", t=PACK),
-        )
         gain = const.tile([P, PACK], F32, name="gain")
         nc.gpsimd.tensor_copy(out=gain[:], in_=gain_col[:])
         shift = const.tile([P, PACK], F32, name="shift")
@@ -156,6 +152,11 @@ def tile_pinmodel_pa_t_kernel(
             if c >= 1:
                 quantise_core(c - 1)
 
+        k1_cols = const.tile([P, DIM], BF16, name="k1_cols")
+        nc.scalar.copy(
+            out=k1_cols[:].rearrange("k (t j) -> k t j", t=PACK),
+            in_=k1_in[:].rearrange("k (j t) -> k t j", t=PACK),
+        )
         b1_cols = const.tile([P, DIM], F32, name="b1_cols")
         nc.scalar.copy(out=b1_cols[:], in_=b1_ps[:])
         fc_bias = const.tile([P, OUT], F32, name="fc_bias")
@@ -340,23 +341,23 @@ def tile_pinmodel_pa_t_kernel(
             if 0 <= i < TILES:
                 stage(i)
 
-        for step in range(-2, TILES + 9):
+        for step in range(-2, TILES + 7):
             at(load_inputs, step + 2 + LOAD_AHEAD)
-            at(transpose_inputs, step + 2)
-            at(transpose_z, step - 5)
-            at(inverse, step - 4)
-            at(normalise, step - 4)
-            at(add_order1, step - 1)
-            at(add_tucker, step - 2)
-            at(finish, step - 8)
-            at(regroup_y, step - 6)
-            at(mean, step - 2)
-            at(quantise_t, step + 1)
-            at(quantise_y, step - 6)
             at(order1_matmul, step)
+            at(transpose_inputs, step + 2)
+            at(transpose_z, step - 4)
+            at(inverse, step - 3)
+            at(normalise, step - 3)
+            at(add_tucker, step - 1)
+            at(finish, step - 7)
+            at(add_order1, step)
+            at(regroup_y, step - 5)
+            at(mean, step - 1)
+            at(quantise_t, step + 1)
+            at(quantise_y, step - 5)
             at(tucker_matmuls, step)
-            at(head_matmul, step - 7)
+            at(head_matmul, step - 6)
             at(evacuate_inputs, step + 2)
-            at(root, step - 3)
-            at(affine, step - 5)
-            at(sum_squares, step - 2)
+            at(root, step - 2)
+            at(affine, step - 4)
+            at(sum_squares, step - 1)

@@ -66,7 +66,8 @@ def tile_pinmodel_pa_t_kernel(
         nc.scalar.activation(out=warm[:], in_=eps[:], func=ACT.Sqrt)
 
         core_in = const.tile([P, PASSES * PACK, DIM], BF16, name="core_in")
-        for c in range(PASSES):
+
+        def load_core(c):
             core = (core2, core3)[c // CORE_PASSES]
             g = c % CORE_PASSES
             halves = core.rearrange("a b d -> (a b) d").rearrange(
@@ -78,7 +79,6 @@ def tile_pinmodel_pa_t_kernel(
             )
 
         k1_in = const.tile([P, DIM], BF16, name="k1_in")
-        nc.sync.dma_start(out=k1_in[:], in_=km1.rearrange("a b d -> (a b) d"))
 
         handed = {}
 
@@ -91,7 +91,13 @@ def tile_pinmodel_pa_t_kernel(
             nc.sync.dma_start(out=x_in[:], in_=x_rows[:, i, :])
             handed["x_in", i] = x_in
 
-        for i in range(LOAD_AHEAD):
+        load_core(0)
+        load_core(1)
+        load_inputs(0)
+        load_core(2)
+        nc.sync.dma_start(out=k1_in[:], in_=km1.rearrange("a b d -> (a b) d"))
+        load_core(3)
+        for i in range(1, LOAD_AHEAD):
             load_inputs(i)
 
         w_words = const.tile([P, OUT], U32, name="w_words", align_bytes=64)
@@ -146,21 +152,9 @@ def tile_pinmodel_pa_t_kernel(
                 in_=core_grouped[:, c, :, :].rearrange("q d v -> q (d v)"),
             )
 
-        for c in range(PASSES + 1):
-            if c < PASSES:
-                regroup_core(c)
-            if c >= 1:
-                quantise_core(c - 1)
-
         k1_cols = const.tile([P, DIM], BF16, name="k1_cols")
-        nc.scalar.copy(
-            out=k1_cols[:].rearrange("k (t j) -> k t j", t=PACK),
-            in_=k1_in[:].rearrange("k (j t) -> k t j", t=PACK),
-        )
         b1_cols = const.tile([P, DIM], F32, name="b1_cols")
-        nc.scalar.copy(out=b1_cols[:], in_=b1_ps[:])
         fc_bias = const.tile([P, OUT], F32, name="fc_bias")
-        nc.scalar.copy(out=fc_bias[:], in_=fcb_ps[:, 0:OUT])
 
         def transpose_inputs(i):
             for name in ("t2", "t3"):
@@ -225,7 +219,7 @@ def tile_pinmodel_pa_t_kernel(
             handed["partial", i] = partial
 
         def add_tucker(i):
-            o = work.tile([P, DIM], F32, name="o", bufs=3)
+            o = work.tile([P, DIM], F32, name="o", bufs=4)
             row_sum = stats.tile([P, 1], F32, name="row_sum")
             nc.vector.scalar_tensor_tensor(
                 out=o[:],
@@ -267,9 +261,9 @@ def tile_pinmodel_pa_t_kernel(
             nc.vector.reciprocal(out=rstd[:], in_=handed["std", i][:])
             handed["rstd", i] = rstd
 
-        def normalise(i):
-            z = work.tile([P, DIM], F32, name="z")
-            nc.gpsimd.tensor_scalar(
+        def normalise(i, engine):
+            z = work.tile([P, DIM], F32, name="z", bufs=3)
+            engine.tensor_scalar(
                 out=z[:],
                 in0=handed["o", i][:],
                 scalar1=handed["neg_mean", i][:],
@@ -279,14 +273,14 @@ def tile_pinmodel_pa_t_kernel(
             )
             handed["z", i] = z
 
-        def transpose_z(i):
-            z_flipped = psum.tile([P, PACK, P], F32, name="z_flipped")
+        def transpose_z(i, bank="z_flipped"):
+            z_flipped = psum.tile([P, PACK, P], F32, name="z_flipped", tag=bank)
             for t in range(PACK):
                 nc.tensor.transpose(z_flipped[:, t, :], handed["z", i][:, P * t : P * (t + 1)], ident_f32[:])
             handed["z_flipped", i] = z_flipped
 
         def affine(i):
-            y_planes = work.tile([P, PACK, P], BF16, name="y_planes")
+            y_planes = work.tile([P, PACK, P], BF16, name="y_planes", bufs=4)
             for t in range(PACK):
                 nc.scalar.activation(
                     out=y_planes[:, t, :],
@@ -298,7 +292,7 @@ def tile_pinmodel_pa_t_kernel(
             handed["y_planes", i] = y_planes
 
         def regroup_y(i):
-            y_grouped = work.tile([P, P, PACK], BF16, name="y_grouped", align_bytes=64)
+            y_grouped = work.tile([P, P, PACK], BF16, name="y_grouped", bufs=3, align_bytes=64)
             nc.vector.tensor_copy(out=y_grouped[:], in_=handed["y_planes", i][:].rearrange("j t r -> j r t"))
             handed["y_grouped", i] = y_grouped
 
@@ -313,8 +307,8 @@ def tile_pinmodel_pa_t_kernel(
             handed["y_codes", i] = y_codes
             handed["y_scales", i] = y_scales
 
-        def head_matmul(i):
-            head = psum.tile([P, OUT], F32, name="head")
+        def head_matmul(i, bank="head"):
+            head = psum.tile([P, OUT], F32, name="head", tag=bank)
             nc.tensor.matmul_mx(
                 out=head[:],
                 lhsT=handed["y_codes", i][:].bitcast(FP8X4),
@@ -337,17 +331,50 @@ def tile_pinmodel_pa_t_kernel(
                     out=out_rows[:, STORE_TILES * group : STORE_TILES * (group + 1), :], in_=result[:]
                 )
 
-        def at(stage, i):
+        def at(stage, i, *rest):
             if 0 <= i < TILES:
-                stage(i)
+                stage(i, *rest)
 
-        for step in range(-2, TILES + 7):
+        def keep_warm(c):
+            for v in range(2):
+                unread = psum.tile([P, DIM], F32, name="unread", tag="z_flipped")
+                nc.tensor.matmul(
+                    out=unread[:], lhsT=ident_bf16[:], rhs=core_in[:, PACK * c + v, :], start=True, stop=True
+                )
+
+        regroup_core(0)
+        nc.scalar.copy(out=b1_cols[:], in_=b1_ps[:])
+        nc.scalar.copy(out=fc_bias[:], in_=fcb_ps[:, 0:OUT])
+        regroup_core(1)
+        quantise_core(0)
+        keep_warm(0)
+        keep_warm(1)
+        transpose_inputs(0)
+        evacuate_inputs(0)
+        regroup_core(2)
+        quantise_core(1)
+        quantise_core(2)
+        quantise_t(0)
+        regroup_core(3)
+        nc.scalar.copy(
+            out=k1_cols[:].rearrange("k (t j) -> k t j", t=PACK),
+            in_=k1_in[:].rearrange("k (j t) -> k t j", t=PACK),
+        )
+        keep_warm(2)
+        keep_warm(3)
+        transpose_inputs(1)
+        evacuate_inputs(1)
+        quantise_core(3)
+        load_inputs(LOAD_AHEAD)
+        load_inputs(LOAD_AHEAD + 1)
+
+        for step in range(TILES - 1):
             at(load_inputs, step + 2 + LOAD_AHEAD)
             at(order1_matmul, step)
             at(transpose_inputs, step + 2)
             at(transpose_z, step - 4)
             at(inverse, step - 3)
-            at(normalise, step - 3)
+            at(normalise, step - 3, nc.gpsimd)
             at(add_tucker, step - 1)
             at(finish, step - 7)
             at(add_order1, step)
@@ -361,3 +388,59 @@ def tile_pinmodel_pa_t_kernel(
             at(root, step - 2)
             at(affine, step - 4)
             at(sum_squares, step - 1)
+
+        n = TILES
+        order1_matmul(n - 1)
+        transpose_z(n - 5)
+        inverse(n - 4)
+        normalise(n - 4, nc.gpsimd)
+        add_tucker(n - 2)
+        add_order1(n - 1)
+        mean(n - 2)
+        tucker_matmuls(n - 1)
+        finish(n - 8)
+        root(n - 3)
+        regroup_y(n - 6)
+        sum_squares(n - 2)
+        affine(n - 5)
+        root(n - 2)
+        inverse(n - 3)
+        quantise_y(n - 6)
+        add_tucker(n - 1)
+        mean(n - 1)
+        head_matmul(n - 7)
+        transpose_z(n - 4)
+        normalise(n - 3, nc.vector)
+        finish(n - 7)
+        inverse(n - 2)
+        sum_squares(n - 1)
+        root(n - 1)
+        affine(n - 4)
+        head_matmul(n - 6)
+        regroup_y(n - 5)
+        normalise(n - 2, nc.vector)
+        transpose_z(n - 3, "t2_flipped")
+        affine(n - 3)
+        quantise_y(n - 5)
+        inverse(n - 1)
+        transpose_z(n - 2, "t3_flipped")
+        finish(n - 6)
+        normalise(n - 1, nc.vector)
+        transpose_z(n - 1)
+        affine(n - 2)
+        affine(n - 1)
+        head_matmul(n - 5, "order1")
+        regroup_y(n - 4)
+        regroup_y(n - 3)
+        quantise_y(n - 4)
+        quantise_y(n - 3)
+        regroup_y(n - 2)
+        head_matmul(n - 4)
+        head_matmul(n - 3, "t2_flipped")
+        regroup_y(n - 1)
+        quantise_y(n - 2)
+        quantise_y(n - 1)
+        head_matmul(n - 2, "t3_flipped")
+        head_matmul(n - 1, "z_flipped")
+        for i in range(n - 5, n):
+            finish(i)

@@ -20,6 +20,7 @@ TILES = ROWS // P
 CORE_PASSES = KR // (P * PACK)
 PASSES = 2 * CORE_PASSES
 LOAD_AHEAD = 4
+X_RUN = 4
 STORE_TILES = 4
 SCALAR_PASS = 1
 
@@ -87,9 +88,10 @@ def tile_pinmodel_pa_t_kernel(
                 t_in = ring.tile([P, KR], BF16, name=name + "_in")
                 nc.sync.dma_start(out=t_in[:], in_=t_rows[name][:, i, :])
                 handed[name + "_in", i] = t_in
-            x_in = ring.tile([P, K1], BF16, name="x_in")
-            nc.sync.dma_start(out=x_in[:], in_=x_rows[:, i, :])
-            handed["x_in", i] = x_in
+            if i % X_RUN == 0:
+                x_in = ring.tile([P, X_RUN, K1], BF16, name="x_in", bufs=3)
+                nc.sync.dma_start(out=x_in[:], in_=x_rows[:, i : i + X_RUN, :])
+                handed["x_in", i // X_RUN] = x_in
 
         load_core(0)
         load_core(1)
@@ -165,9 +167,13 @@ def tile_pinmodel_pa_t_kernel(
                         first = P * (2 * g + u)
                         nc.tensor.transpose(flipped[:, g, u, :], pairs[:, first : first + P], ident_f32[:])
                 handed[name + "_flipped", i] = flipped
-            x_flipped = psum.tile([P, P], BF16, name="x_flipped")
-            nc.tensor.transpose(x_flipped[:], handed["x_in", i][:], ident_bf16[:])
-            handed["x_flipped", i] = x_flipped
+            if i % X_RUN == 0:
+                x_flipped = psum.tile([P, X_RUN, P], BF16, name="x_flipped")
+                for place in range(X_RUN):
+                    nc.tensor.transpose(
+                        x_flipped[:, place, :], handed["x_in", i // X_RUN][:, place, :], ident_bf16[:]
+                    )
+                handed["x_flipped", i // X_RUN] = x_flipped
 
         def evacuate_inputs(i):
             t_grouped = work.tile([P, PASSES, P, PACK], BF16, name="t_grouped", bufs=3, align_bytes=64)
@@ -178,9 +184,10 @@ def tile_pinmodel_pa_t_kernel(
                     in_=handed[name + "_flipped", i][:].rearrange("q g u r -> q g r u"),
                 )
             handed["t_grouped", i] = t_grouped
-            x_cols = work.tile([P, P], BF16, name="x_cols", bufs=3)
-            nc.scalar.copy(out=x_cols[:], in_=handed["x_flipped", i][:])
-            handed["x_cols", i] = x_cols
+            if i % X_RUN == 0:
+                x_cols = work.tile([P, X_RUN, P], BF16, name="x_cols")
+                nc.scalar.copy(out=x_cols[:], in_=handed["x_flipped", i // X_RUN][:])
+                handed["x_cols", i // X_RUN] = x_cols
 
         def quantise_t(i):
             t_codes = work.tile([P, PASSES * P], U32, name="t_codes", align_bytes=64)
@@ -210,7 +217,7 @@ def tile_pinmodel_pa_t_kernel(
 
         def order1_matmul(i):
             order1 = psum.tile([P, DIM], F32, name="order1")
-            nc.tensor.matmul(out=order1[:], lhsT=handed["x_cols", i][:], rhs=k1_cols[:], start=True, stop=True)
+            nc.tensor.matmul(out=order1[:], lhsT=handed["x_cols", i // X_RUN][:, i % X_RUN, :], rhs=k1_cols[:], start=True, stop=True)
             handed["order1", i] = order1
 
         def add_order1(i):
@@ -233,9 +240,9 @@ def tile_pinmodel_pa_t_kernel(
             handed["o", i] = o
             handed["row_sum", i] = row_sum
 
-        def mean(i):
+        def mean(i, engine):
             neg_mean = stats.tile([P, 1], F32, name="neg_mean")
-            nc.vector.tensor_scalar_mul(out=neg_mean[:], in0=handed["row_sum", i][:], scalar1=-1.0 / DIM)
+            engine.tensor_scalar_mul(out=neg_mean[:], in0=handed["row_sum", i][:], scalar1=-1.0 / DIM)
             handed["neg_mean", i] = neg_mean
 
         def sum_squares(i):
@@ -379,7 +386,7 @@ def tile_pinmodel_pa_t_kernel(
             at(finish, step - 7)
             at(add_order1, step)
             at(regroup_y, step - 5)
-            at(mean, step - 1)
+            at(mean, step - 1, nc.gpsimd)
             at(quantise_t, step + 1)
             at(quantise_y, step - 5)
             at(tucker_matmuls, step)
@@ -396,7 +403,7 @@ def tile_pinmodel_pa_t_kernel(
         normalise(n - 4, nc.gpsimd)
         add_tucker(n - 2)
         add_order1(n - 1)
-        mean(n - 2)
+        mean(n - 2, nc.vector)
         tucker_matmuls(n - 1)
         finish(n - 8)
         root(n - 3)
@@ -407,7 +414,7 @@ def tile_pinmodel_pa_t_kernel(
         inverse(n - 3)
         quantise_y(n - 6)
         add_tucker(n - 1)
-        mean(n - 1)
+        mean(n - 1, nc.vector)
         head_matmul(n - 7)
         transpose_z(n - 4)
         normalise(n - 3, nc.vector)

@@ -34,7 +34,7 @@ def tile_pinmodel_pa_t_kernel(
     with ExitStack() as ctx:
         ctx.enter_context(tc.manual_schedule())
         const = ctx.enter_context(tc.tile_pool(name="const", bufs=1))
-        ring = ctx.enter_context(tc.tile_pool(name="ring", bufs=LOAD_AHEAD + 1))
+        ring = ctx.enter_context(tc.tile_pool(name="ring", bufs=LOAD_AHEAD + 2))
         work = ctx.enter_context(tc.tile_pool(name="work", bufs=2))
         stats = ctx.enter_context(tc.tile_pool(name="stats", bufs=4))
         psum = ctx.enter_context(tc.psum_pool(name="psum", bufs=1))
@@ -56,13 +56,9 @@ def tile_pinmodel_pa_t_kernel(
         nc.vector.memset(w_scales[:].bitcast(I32), 0)
 
         b1_col = const.tile([P, PACK], BF16, name="b1_col")
-        nc.scalar.dma_start(out=b1_col[:], in_=b1.rearrange("(j t) -> j t", t=PACK))
         fcb_col = const.tile([P, 1], BF16, name="fcb_col")
-        nc.scalar.dma_start(out=fcb_col[:], in_=fc_b.rearrange("(n o) -> n o", o=1))
         gain_col = const.tile([P, PACK], BF16, name="gain_col")
-        nc.scalar.dma_start(out=gain_col[:], in_=ln_g.rearrange("(j t) -> j t", t=PACK))
         shift_col = const.tile([P, PACK], BF16, name="shift_col")
-        nc.scalar.dma_start(out=shift_col[:], in_=ln_b.rearrange("(j t) -> j t", t=PACK))
         warm = const.tile([P, 1], F32, name="warm")
         nc.scalar.activation(out=warm[:], in_=eps[:], func=ACT.Sqrt)
 
@@ -99,8 +95,13 @@ def tile_pinmodel_pa_t_kernel(
         load_core(2)
         nc.sync.dma_start(out=k1_in[:], in_=km1.rearrange("a b d -> (a b) d"))
         load_core(3)
-        for i in range(1, LOAD_AHEAD):
+        load_inputs(1)
+        nc.sync.dma_start(out=b1_col[:], in_=b1.rearrange("(j t) -> j t", t=PACK))
+        for i in range(2, LOAD_AHEAD + 2):
             load_inputs(i)
+        nc.sync.dma_start(out=gain_col[:], in_=ln_g.rearrange("(j t) -> j t", t=PACK))
+        nc.sync.dma_start(out=shift_col[:], in_=ln_b.rearrange("(j t) -> j t", t=PACK))
+        nc.sync.dma_start(out=fcb_col[:], in_=fc_b.rearrange("(n o) -> n o", o=1))
 
         w_words = const.tile([P, OUT], U32, name="w_words", align_bytes=64)
         nc.sync.dma_start(
@@ -118,23 +119,17 @@ def tile_pinmodel_pa_t_kernel(
         shift = const.tile([P, PACK], F32, name="shift")
         nc.gpsimd.tensor_copy(out=shift[:], in_=shift_col[:])
 
-        b1_ps = psum.tile([P, DIM], F32, name="acc", bufs=2)
-        for t in range(PACK):
-            nc.tensor.matmul(
-                out=b1_ps[:, P * t : P * (t + 1)],
-                lhsT=b1_col[:, t : t + 1].to_broadcast([P, P]),
-                rhs=ident_bf16[:],
-                start=True,
-                stop=True,
-            )
-        fcb_ps = psum.tile([P, DIM], F32, name="acc", bufs=2)
-        nc.tensor.matmul(
-            out=fcb_ps[:, 0:OUT],
-            lhsT=fcb_col[:, 0:1].to_broadcast([P, P]),
-            rhs=ident_bf16[:],
-            start=True,
-            stop=True,
-        )
+        def spread(columns, out):
+            spread_ps = psum.tile([P, DIM], F32, name="spread", tag="head")
+            for t in range(columns.shape[1]):
+                nc.tensor.matmul(
+                    out=spread_ps[:, P * t : P * (t + 1)],
+                    lhsT=columns[:, t : t + 1].to_broadcast([P, P]),
+                    rhs=ident_bf16[:],
+                    start=True,
+                    stop=True,
+                )
+            nc.scalar.copy(out=out, in_=spread_ps[:, 0 : P * columns.shape[1]])
 
         core_grouped = const.tile([P, PASSES, DIM, PACK], BF16, name="core_grouped", align_bytes=64)
         core_codes = const.tile([P, PASSES, DIM], U32, name="core_codes", align_bytes=64)
@@ -350,8 +345,6 @@ def tile_pinmodel_pa_t_kernel(
                 )
 
         regroup_core(0)
-        nc.scalar.copy(out=b1_cols[:], in_=b1_ps[:])
-        nc.scalar.copy(out=fc_bias[:], in_=fcb_ps[:, 0:OUT])
         regroup_core(1)
         quantise_core(0)
         keep_warm(0)
@@ -371,12 +364,13 @@ def tile_pinmodel_pa_t_kernel(
         keep_warm(3)
         transpose_inputs(1)
         evacuate_inputs(1)
+        spread(b1_col, b1_cols[:])
         quantise_core(3)
-        load_inputs(LOAD_AHEAD)
-        load_inputs(LOAD_AHEAD + 1)
 
         for step in range(TILES - 1):
             at(load_inputs, step + 2 + LOAD_AHEAD)
+            if step == 3:
+                spread(fcb_col, fc_bias[:])
             at(order1_matmul, step)
             at(transpose_inputs, step + 2)
             at(transpose_z, step - 4)

from contextlib import ExitStack

import concourse.mybir as mybir
from concourse.masks import make_identity

F32 = mybir.dt.float32
BF16 = mybir.dt.bfloat16
U32 = mybir.dt.uint32
U8 = mybir.dt.uint8
I32 = mybir.dt.int32
FP8X4 = mybir.dt.float8_e4m3fn_x4
ACT = mybir.ActivationFunctionType
ALU = mybir.AluOpType

P = 128
PACK = 4
ROWS, K1, KR, DIM, OUT = 4096, 128, 1024, 512, 128
EPS = 1e-5
TILES = ROWS // P
CORE_PASSES = KR // (P * PACK)
PASSES = 2 * CORE_PASSES
LOAD_AHEAD = 4
X_RUN = 4
STORE_TILES = 4
SCALAR_PASS = 1

FLOPS = 2 * ROWS * (K1 * DIM + 2 * KR * DIM + DIM * OUT)


def tile_pinmodel_pa_t_kernel(
    tc, x, km1, b1, t2, core2, t3, core3, ln_g, ln_b, fc_w_words, fc_w_scales, fc_b, out
):
    nc = tc.nc
    with ExitStack() as ctx:
        ctx.enter_context(tc.manual_schedule())
        const = ctx.enter_context(tc.tile_pool(name="const", bufs=1))
        ring = ctx.enter_context(tc.tile_pool(name="ring", bufs=LOAD_AHEAD + 2))
        work = ctx.enter_context(tc.tile_pool(name="work", bufs=2))
        stats = ctx.enter_context(tc.tile_pool(name="stats", bufs=4))
        psum = ctx.enter_context(tc.psum_pool(name="psum", bufs=1))

        x_rows = x.rearrange("(p i) a b -> p i (a b)", i=TILES)
        t_rows = {
            "t2": t2.rearrange("(p i) a b -> p i (a b)", i=TILES),
            "t3": t3.rearrange("(p i) a b -> p i (a b)", i=TILES),
        }
        out_rows = out.rearrange("(p i) o c -> p i (o c)", i=TILES)

        ident_f32 = const.tile([P, P], F32, name="ident_f32")
        make_identity(nc, ident_f32[:])
        ident_bf16 = const.tile([P, P], BF16, name="ident_bf16")
        make_identity(nc, ident_bf16[:])
        eps = const.tile([P, 1], F32, name="eps")
        nc.vector.memset(eps[:], EPS)
        w_scales = const.tile([P, OUT], U8, name="w_scales", align_bytes=64)
        nc.vector.memset(w_scales[:].bitcast(I32), 0)

        b1_col = const.tile([P, PACK], BF16, name="b1_col")
        fcb_col = const.tile([P, 1], BF16, name="fcb_col")
        gain_col = const.tile([P, PACK], BF16, name="gain_col")
        shift_col = const.tile([P, PACK], BF16, name="shift_col")
        warm = const.tile([P, 1], F32, name="warm")
        nc.scalar.activation(out=warm[:], in_=eps[:], func=ACT.Sqrt)

        core_in = const.tile([P, PASSES * PACK, DIM], BF16, name="core_in")

        def load_core(c):
            core = (core2, core3)[c // CORE_PASSES]
            g = c % CORE_PASSES
            halves = core.rearrange("a b d -> (a b) d").rearrange(
                "(h q e) d -> q h (e d)", q=P, e=2
            )
            nc.sync.dma_start(
                out=core_in[:, PACK * c : PACK * (c + 1), :].rearrange("q (u e) d -> q u (e d)", e=2),
                in_=halves[:, 2 * g : 2 * g + 2, :],
            )

        k1_in = const.tile([P, DIM], BF16, name="k1_in")

        handed = {}

        def load_inputs(i):
            for name in ("t2", "t3"):
                t_in = ring.tile([P, KR], BF16, name=name + "_in")
                nc.sync.dma_start(out=t_in[:], in_=t_rows[name][:, i, :])
                handed[name + "_in", i] = t_in
            if i % X_RUN == 0:
                x_in = ring.tile([P, X_RUN, K1], BF16, name="x_in", bufs=3)
                nc.sync.dma_start(out=x_in[:], in_=x_rows[:, i : i + X_RUN, :])
                handed["x_in", i // X_RUN] = x_in

        load_core(0)
        load_core(1)
        load_inputs(0)
        load_core(2)
        nc.sync.dma_start(out=k1_in[:], in_=km1.rearrange("a b d -> (a b) d"))
        load_core(3)
        load_inputs(1)
        nc.sync.dma_start(out=b1_col[:], in_=b1.rearrange("(j t) -> j t", t=PACK))
        for i in range(2, LOAD_AHEAD + 2):
            load_inputs(i)
        nc.sync.dma_start(out=gain_col[:], in_=ln_g.rearrange("(j t) -> j t", t=PACK))
        nc.sync.dma_start(out=shift_col[:], in_=ln_b.rearrange("(j t) -> j t", t=PACK))
        nc.sync.dma_start(out=fcb_col[:], in_=fc_b.rearrange("(n o) -> n o", o=1))

        w_words = const.tile([P, OUT], U32, name="w_words", align_bytes=64)
        nc.sync.dma_start(
            out=w_words[:].bitcast(I32),
            in_=fc_w_words[0].rearrange("p n t -> p (n t)").bitcast(I32),
        )
        for quadrant in range(4):
            nc.sync.dma_start(
                out=w_scales[32 * quadrant : 32 * quadrant + 4, :].bitcast(I32),
                in_=fc_w_scales[0, 4 * quadrant : 4 * quadrant + 4, :].bitcast(I32),
            )

        gain = const.tile([P, PACK], F32, name="gain")
        nc.gpsimd.tensor_copy(out=gain[:], in_=gain_col[:])
        shift = const.tile([P, PACK], F32, name="shift")
        nc.gpsimd.tensor_copy(out=shift[:], in_=shift_col[:])

        def spread(columns, out):
            spread_ps = psum.tile([P, DIM], F32, name="spread", tag="head")
            for t in range(columns.shape[1]):
                nc.tensor.matmul(
                    out=spread_ps[:, P * t : P * (t + 1)],
                    lhsT=columns[:, t : t + 1].to_broadcast([P, P]),
                    rhs=ident_bf16[:],
                    start=True,
                    stop=True,
                )
            nc.scalar.copy(out=out, in_=spread_ps[:, 0 : P * columns.shape[1]])

        core_grouped = const.tile([P, PASSES, DIM, PACK], BF16, name="core_grouped", align_bytes=64)
        core_codes = const.tile([P, PASSES, DIM], U32, name="core_codes", align_bytes=64)
        core_scales = const.tile([P, PASSES, DIM], U8, name="core_scales", align_bytes=64)

        def regroup_core(c):
            copy = nc.scalar.copy if c == SCALAR_PASS else nc.vector.tensor_copy
            copy(
                out=core_grouped[:, c, :, :].rearrange("q (t j) v -> q j v t", t=PACK),
                in_=core_in[:, PACK * c : PACK * (c + 1), :].rearrange("q v (j t) -> q j v t", t=PACK),
            )

        def quantise_core(c):
            nc.vector.quantize_mx(
                out=core_codes[:, c, :].bitcast(FP8X4),
                scales=core_scales[:, c, :],
                in_=core_grouped[:, c, :, :].rearrange("q d v -> q (d v)"),
            )

        k1_cols = const.tile([P, DIM], BF16, name="k1_cols")
        b1_cols = const.tile([P, DIM], F32, name="b1_cols")
        fc_bias = const.tile([P, OUT], F32, name="fc_bias")

        def transpose_inputs(i):
            for name in ("t2", "t3"):
                pairs = handed[name + "_in", i][:].bitcast(F32)
                flipped = psum.tile([P, CORE_PASSES, 2, P], F32, name=name + "_flipped")
                for g in range(CORE_PASSES):
                    for u in range(2):
                        first = P * (2 * g + u)
                        nc.tensor.transpose(flipped[:, g, u, :], pairs[:, first : first + P], ident_f32[:])
                handed[name + "_flipped", i] = flipped
            if i % X_RUN == 0:
                x_flipped = psum.tile([P, X_RUN, P], BF16, name="x_flipped")
                for place in range(X_RUN):
                    nc.tensor.transpose(
                        x_flipped[:, place, :], handed["x_in", i // X_RUN][:, place, :], ident_bf16[:]
                    )
                handed["x_flipped", i // X_RUN] = x_flipped

        def evacuate_inputs(i):
            t_grouped = work.tile([P, PASSES, P, PACK], BF16, name="t_grouped", bufs=3, align_bytes=64)
            pairs = t_grouped[:].bitcast(F32)
            for first, name in ((0, "t2"), (CORE_PASSES, "t3")):
                nc.scalar.copy(
                    out=pairs[:, first : first + CORE_PASSES],
                    in_=handed[name + "_flipped", i][:].rearrange("q g u r -> q g r u"),
                )
            handed["t_grouped", i] = t_grouped
            if i % X_RUN == 0:
                x_cols = work.tile([P, X_RUN, P], BF16, name="x_cols")
                nc.scalar.copy(out=x_cols[:], in_=handed["x_flipped", i // X_RUN][:])
                handed["x_cols", i // X_RUN] = x_cols

        def quantise_t(i):
            t_codes = work.tile([P, PASSES * P], U32, name="t_codes", align_bytes=64)
            t_scales = work.tile([P, PASSES * P], U8, name="t_scales", align_bytes=64)
            nc.vector.quantize_mx(
                out=t_codes[:].bitcast(FP8X4),
                scales=t_scales[:],
                in_=handed["t_grouped", i][:].rearrange("q c r v -> q (c r v)"),
            )
            handed["t_codes", i] = t_codes
            handed["t_scales", i] = t_scales

        def tucker_matmuls(i):
            acc = psum.tile([P, DIM], F32, name="acc", bufs=2)
            for c in range(PASSES):
                samples = slice(P * c, P * (c + 1))
                nc.tensor.matmul_mx(
                    out=acc[:],
                    lhsT=handed["t_codes", i][:, samples].bitcast(FP8X4),
                    lhsT_scale=handed["t_scales", i][:, samples],
                    rhs=core_codes[:, c, :].bitcast(FP8X4),
                    rhs_scale=core_scales[:, c, :],
                    start=(c == 0),
                    stop=(c == PASSES - 1),
                )
            handed["acc", i] = acc

        def order1_matmul(i):
            order1 = psum.tile([P, DIM], F32, name="order1")
            nc.tensor.matmul(out=order1[:], lhsT=handed["x_cols", i // X_RUN][:, i % X_RUN, :], rhs=k1_cols[:], start=True, stop=True)
            handed["order1", i] = order1

        def add_order1(i):
            partial = work.tile([P, DIM], F32, name="partial")
            nc.vector.tensor_tensor(out=partial[:], in0=handed["order1", i][:], in1=b1_cols[:], op=ALU.add)
            handed["partial", i] = partial

        def add_tucker(i):
            o = work.tile([P, DIM], F32, name="o", bufs=4)
            row_sum = stats.tile([P, 1], F32, name="row_sum")
            nc.vector.scalar_tensor_tensor(
                out=o[:],
                in0=handed["acc", i][:],
                scalar=1.0,
                in1=handed["partial", i][:],
                op0=ALU.mult,
                op1=ALU.add,
                accum_out=row_sum[:],
            )
            handed["o", i] = o
            handed["row_sum", i] = row_sum

        def mean(i, engine):
            neg_mean = stats.tile([P, 1], F32, name="neg_mean")
            engine.tensor_scalar_mul(out=neg_mean[:], in0=handed["row_sum", i][:], scalar1=-1.0 / DIM)
            handed["neg_mean", i] = neg_mean

        def sum_squares(i):
            squares = work.tile([P, DIM], BF16, name="squares")
            sum_sq = stats.tile([P, 1], F32, name="sum_sq")
            nc.scalar.activation(
                out=squares[:],
                in_=handed["o", i][:],
                func=ACT.Square,
                bias=handed["neg_mean", i][:],
                scale=1.0,
                accum_out=sum_sq[:],
            )
            handed["sum_sq", i] = sum_sq

        def root(i):
            std = stats.tile([P, 1], F32, name="std")
            nc.scalar.activation(out=std[:], in_=handed["sum_sq", i][:], func=ACT.Sqrt, bias=eps[:], scale=1.0 / DIM)
            handed["std", i] = std

        def inverse(i):
            rstd = stats.tile([P, 1], F32, name="rstd")
            nc.vector.reciprocal(out=rstd[:], in_=handed["std", i][:])
            handed["rstd", i] = rstd

        def normalise(i, engine):
            z = work.tile([P, DIM], F32, name="z", bufs=3)
            engine.tensor_scalar(
                out=z[:],
                in0=handed["o", i][:],
                scalar1=handed["neg_mean", i][:],
                scalar2=handed["rstd", i][:],
                op0=ALU.add,
                op1=ALU.mult,
            )
            handed["z", i] = z

        def transpose_z(i, bank="z_flipped"):
            z_flipped = psum.tile([P, PACK, P], F32, name="z_flipped", tag=bank)
            for t in range(PACK):
                nc.tensor.transpose(z_flipped[:, t, :], handed["z", i][:, P * t : P * (t + 1)], ident_f32[:])
            handed["z_flipped", i] = z_flipped

        def affine(i):
            y_planes = work.tile([P, PACK, P], BF16, name="y_planes", bufs=4)
            for t in range(PACK):
                nc.scalar.activation(
                    out=y_planes[:, t, :],
                    in_=handed["z_flipped", i][:, t, :],
                    func=ACT.Identity,
                    bias=shift[:, t : t + 1],
                    scale=gain[:, t : t + 1],
                )
            handed["y_planes", i] = y_planes

        def regroup_y(i):
            y_grouped = work.tile([P, P, PACK], BF16, name="y_grouped", bufs=3, align_bytes=64)
            nc.vector.tensor_copy(out=y_grouped[:], in_=handed["y_planes", i][:].rearrange("j t r -> j r t"))
            handed["y_grouped", i] = y_grouped

        def quantise_y(i):
            y_codes = work.tile([P, P], U32, name="y_codes", bufs=3, align_bytes=64)
            y_scales = work.tile([P, P], U8, name="y_scales", bufs=3, align_bytes=64)
            nc.vector.quantize_mx(
                out=y_codes[:].bitcast(FP8X4),
                scales=y_scales[:],
                in_=handed["y_grouped", i][:].rearrange("j r t -> j (r t)"),
            )
            handed["y_codes", i] = y_codes
            handed["y_scales", i] = y_scales

        def head_matmul(i, bank="head"):
            head = psum.tile([P, OUT], F32, name="head", tag=bank)
            nc.tensor.matmul_mx(
                out=head[:],
                lhsT=handed["y_codes", i][:].bitcast(FP8X4),
                lhsT_scale=handed["y_scales", i][:],
                rhs=w_words[:].bitcast(FP8X4),
                rhs_scale=w_scales[:],
                start=True,
                stop=True,
            )
            handed["head", i] = head

        def finish(i):
            group, place = divmod(i, STORE_TILES)
            if place == 0:
                handed["result", group] = work.tile([P, STORE_TILES, OUT], F32, name="result")
            result = handed["result", group]
            nc.vector.tensor_tensor(out=result[:, place, :], in0=handed["head", i][:], in1=fc_bias[:], op=ALU.add)
            if place == STORE_TILES - 1:
                nc.sync.dma_start(
                    out=out_rows[:, STORE_TILES * group : STORE_TILES * (group + 1), :], in_=result[:]
                )

        def at(stage, i, *rest):
            if 0 <= i < TILES:
                stage(i, *rest)

        def keep_warm(c):
            for v in range(2):
                unread = psum.tile([P, DIM], F32, name="unread", tag="z_flipped")
                nc.tensor.matmul(
                    out=unread[:], lhsT=ident_bf16[:], rhs=core_in[:, PACK * c + v, :], start=True, stop=True
                )

        regroup_core(0)
        regroup_core(1)
        quantise_core(0)
        keep_warm(0)
        keep_warm(1)
        transpose_inputs(0)
        evacuate_inputs(0)
        regroup_core(2)
        quantise_core(1)
        quantise_core(2)
        quantise_t(0)
        regroup_core(3)
        nc.scalar.copy(
            out=k1_cols[:].rearrange("k (t j) -> k t j", t=PACK),
            in_=k1_in[:].rearrange("k (j t) -> k t j", t=PACK),
        )
        keep_warm(2)
        keep_warm(3)
        transpose_inputs(1)
        evacuate_inputs(1)
        spread(b1_col, b1_cols[:])
        quantise_core(3)

        for step in range(TILES - 1):
            at(load_inputs, step + 2 + LOAD_AHEAD)
            if step == 3:
                spread(fcb_col, fc_bias[:])
            at(order1_matmul, step)
            at(transpose_inputs, step + 2)
            at(transpose_z, step - 4)
            at(inverse, step - 3)
            at(normalise, step - 3, nc.gpsimd)
            at(add_tucker, step - 1)
            at(finish, step - 7)
            at(add_order1, step)
            at(regroup_y, step - 5)
            at(mean, step - 1, nc.gpsimd)
            at(quantise_t, step + 1)
            at(quantise_y, step - 5)
            at(tucker_matmuls, step)
            at(head_matmul, step - 6)
            at(evacuate_inputs, step + 2)
            at(root, step - 2)
            at(affine, step - 4)
            at(sum_squares, step - 1)

        n = TILES
        order1_matmul(n - 1)
        transpose_z(n - 5)
        inverse(n - 4)
        normalise(n - 4, nc.gpsimd)
        add_tucker(n - 2)
        add_order1(n - 1)
        mean(n - 2, nc.vector)
        tucker_matmuls(n - 1)
        finish(n - 8)
        root(n - 3)
        regroup_y(n - 6)
        sum_squares(n - 2)
        affine(n - 5)
        root(n - 2)
        inverse(n - 3)
        quantise_y(n - 6)
        add_tucker(n - 1)
        mean(n - 1, nc.vector)
        head_matmul(n - 7)
        transpose_z(n - 4)
        normalise(n - 3, nc.vector)
        finish(n - 7)
        inverse(n - 2)
        sum_squares(n - 1)
        root(n - 1)
        affine(n - 4)
        head_matmul(n - 6)
        regroup_y(n - 5)
        normalise(n - 2, nc.vector)
        transpose_z(n - 3, "t2_flipped")
        affine(n - 3)
        quantise_y(n - 5)
        inverse(n - 1)
        transpose_z(n - 2, "t3_flipped")
        finish(n - 6)
        normalise(n - 1, nc.vector)
        transpose_z(n - 1)
        affine(n - 2)
        affine(n - 1)
        head_matmul(n - 5, "order1")
        regroup_y(n - 4)
        regroup_y(n - 3)
        quantise_y(n - 4)
        quantise_y(n - 3)
        regroup_y(n - 2)
        head_matmul(n - 4)
        head_matmul(n - 3, "t2_flipped")
        regroup_y(n - 1)
        quantise_y(n - 2)
        quantise_y(n - 1)
        head_matmul(n - 2, "t3_flipped")
        head_matmul(n - 1, "z_flipped")
        for i in range(n - 5, n):
            finish(i)
